import numpy as np
import ml_dtypes


def mxq(x, axis, fmt="e4m3"):
    dtype, down = {"e4m3": (ml_dtypes.float8_e4m3fn, 7), "e5m2": (ml_dtypes.float8_e5m2, 14)}[fmt]
    v = np.moveaxis(np.asarray(x, np.float32).astype(ml_dtypes.bfloat16).astype(np.float64), axis, -1)
    blocks = v.reshape(v.shape[:-1] + (-1, 32))
    amax = np.abs(blocks).max(-1, keepdims=True)
    byte = np.maximum(np.where(amax > 0, np.frexp(amax)[1] - 1 + 127, 0) - down, 1)
    scale = np.exp2(byte - 127.0)
    codes = (blocks / scale).astype(np.float32).astype(dtype).astype(np.float64)
    return np.moveaxis((codes * scale).reshape(v.shape), -1, axis)


WIDE = False


def mx_kscale(k):
    if not WIDE:
        return np.ones(k)
    levels = np.array([10, -10, 5, -5, 0])
    a = np.random.permutation(np.resize(levels, k // 512 * 4)).reshape(k // 512, 4)
    idx = np.arange(k)
    return np.exp2(a[idx // 512, idx % 128 // 32])


BF16 = ml_dtypes.bfloat16


def bf(x):
    return np.asarray(x, np.float32).astype(BF16)


def f64(x):
    return np.asarray(x).astype(np.float64)


B, D, P, C, DEPTH = 512, 1024, 512, 128, 5
INT = (1 << DEPTH) - 1
TOT = INT + INT + 1
SIGMA = 1.0


def path_probs(th):
    prob = np.ones((1, th.shape[1]))
    probs = [prob]
    off = 0
    for d in range(DEPTH):
        n = 1 << d
        t = th[off:off + n]
        left = prob * (1.0 + t) * 0.5
        right = prob * (1.0 - t) * 0.5
        prob = np.stack([left, right], axis=1).reshape(n + n, -1)
        probs.append(prob)
        off += n
    return np.concatenate(probs, axis=0)


def setup_inputs():
    s, t = mx_kscale(D), mx_kscale(P)
    return {"X": bf(np.random.standard_normal((B, D)) * s),
            "Z": bf(np.random.standard_normal((P, D)) * 0.25 * P / np.sqrt(D) * t[:, None] / s),
            "W": bf(np.random.standard_normal((C * TOT, P)) * 4.0 / np.sqrt(P) / t),
            "V": bf(np.random.standard_normal((C * TOT, P)) * 4.0 / np.sqrt(P) / t),
            "th": bf(np.tanh(1.5 * np.random.standard_normal((INT, B))))}


def reference(X, Z, W, V, th):
    Xp = (mxq(f64(Z), 1, "e4m3") @ mxq(f64(X), 1, "e4m3").T) / P
    Xq = mxq(Xp, 0, "e4m3")
    WX = (mxq(f64(W), 1, "e4m3") @ Xq).reshape(TOT, C, B)
    VX = (mxq(f64(V), 1, "e4m3") @ Xq).reshape(TOT, C, B)
    probs = path_probs(f64(th))
    return np.sum(probs[:, None, :] * WX * np.tanh(SIGMA * VX), axis=0)

@@ -1,0 +1,310 @@
+from contextlib import ExitStack
+
+import concourse.mybir as mybir
+from concourse.masks import make_identity
+
+F32 = mybir.dt.float32
+BF16 = mybir.dt.bfloat16
+U32 = mybir.dt.uint32
+U8 = mybir.dt.uint8
+FP8X4 = mybir.dt.float8_e4m3fn_x4
+ADD = mybir.AluOpType.add
+MULT = mybir.AluOpType.mult
+TANH = mybir.ActivationFunctionType.Tanh
+
+P = 128
+PACK = 4
+K_PASS = P * PACK
+HALVES = 2
+
+SAMPLES, FEATURES, PROJECTED, CLASSES = 512, 1024, 512, 128
+DEPTH = 5
+INNER_NODES = (1 << DEPTH) - 1
+NODES = 2 * INNER_NODES + 1
+SAMPLE_TILES = SAMPLES // P
+FEATURE_PASSES = FEATURES // K_PASS
+GROUP_NODES = 4
+BANK_BLOCKS = 2
+
+DIRECT_TILES = 2
+RAW_BUFS = 6
+
+FLOPS = 2 * PROJECTED * SAMPLES * FEATURES + 2 * 2 * NODES * CLASSES * SAMPLES * PROJECTED
+
+
+def node_groups():
+    groups = []
+    first = 0
+    for size in (GROUP_NODES, 2, 1):
+        for repeat in range((NODES - first) // size):
+            groups.append((first, size))
+            first += size
+    return groups
+
+
+def tile_bonsailayer_pa_kernel(tc, X, Z, W, V, th, out):
+    nc = tc.nc
+    groups = node_groups()
+
+    with ExitStack() as ctx:
+        consts = ctx.enter_context(tc.tile_pool(name="consts", bufs=1))
+        first_stage = ctx.enter_context(tc.tile_pool(name="first_stage", bufs=4))
+        raw_pool = ctx.enter_context(tc.tile_pool(name="raw", bufs=RAW_BUFS))
+        grouped_pool = ctx.enter_context(tc.tile_pool(name="grouped", bufs=3))
+        codes_pool = ctx.enter_context(tc.tile_pool(name="codes", bufs=3))
+        work = ctx.enter_context(tc.tile_pool(name="work", bufs=4))
+        psum_words = ctx.enter_context(tc.psum_pool(name="psum_words", bufs=3))
+        psum_products = ctx.enter_context(tc.psum_pool(name="psum_products", bufs=2))
+        psum_score = ctx.enter_context(tc.psum_pool(name="psum_score", bufs=1))
+        ctx.enter_context(tc.manual_schedule())
+
+        ident_f32 = consts.tile([P, P], F32, name="ident_f32")
+        make_identity(nc, ident_f32[:])
+        ident_bf16 = consts.tile([P, P], BF16, name="ident_bf16")
+        make_identity(nc, ident_bf16[:])
+
+        th_rows = consts.tile([P, SAMPLES], BF16, name="th_rows")
+        nc.vector.memset(th_rows[:], 0.0)
+        nc.scalar.dma_start(out=th_rows[:INNER_NODES, :], in_=th)
+
+        warm = consts.tile([P, 1], F32, name="warm")
+        nc.vector.memset(warm[:], 0.0)
+        nc.scalar.activation(out=warm[:], in_=warm[:], func=TANH)
+
+        z_raw = consts.tile([P, PACK * FEATURES], BF16, name="z_raw")
+        for u in range(HALVES):
+            nc.sync.dma_start(
+                out=z_raw[:, u * 2 * FEATURES : (u + 1) * 2 * FEATURES],
+                in_=Z[u * 2 * P : (u + 1) * 2 * P, :].rearrange("(q e) d -> q (e d)", e=2),
+            )
+        x_raw = consts.tile([P, SAMPLE_TILES * FEATURES], BF16, name="x_raw")
+        for s in range(SAMPLE_TILES):
+            nc.sync.dma_start(
+                out=x_raw[:, s * FEATURES : (s + 1) * FEATURES], in_=X[s * P : (s + 1) * P, :]
+            )
+
+        def transpose_blocks(words, blocks, grouped_words, copy):
+            bank = psum_words.tile([P, BANK_BLOCKS, HALVES, P], F32, name="bank", tag="bank")
+            for a in range(blocks):
+                for u in range(HALVES):
+                    first_word = (a * HALVES + u) * P
+                    nc.tensor.transpose(
+                        bank[:, a, u, :], words[:, first_word : first_word + P], ident_f32[:]
+                    )
+            copy(
+                out=grouped_words.rearrange("q (a r u) -> q a r u", a=blocks, u=HALVES),
+                in_=bank[:, :blocks].rearrange("q a u r -> q a r u"),
+            )
+
+        def quantise(grouped, codes, scales):
+            nc.vector.quantize_mx(out=codes.bitcast(FP8X4), scales=scales, in_=grouped)
+
+        def quantise_row_tiles(raw, name):
+            codes = consts.tile([P, PACK * FEATURE_PASSES * P], U32, name=name + "_codes", align_bytes=64)
+            scales = consts.tile([P, PACK * FEATURE_PASSES * P], U8, name=name + "_scales", align_bytes=64)
+            words = raw[:].bitcast(F32)
+            row_words = FEATURES // 2
+            grouped_tiles = []
+            for r in range(PACK):
+                grouped = first_stage.tile([P, FEATURES], BF16, name=name + "_grouped", tag="grouped", align_bytes=64)
+                copy = nc.scalar.copy if r % 2 == 0 else nc.vector.tensor_copy
+                transpose_blocks(
+                    words[:, r * row_words : (r + 1) * row_words],
+                    FEATURE_PASSES,
+                    grouped[:].bitcast(F32),
+                    copy,
+                )
+                grouped_tiles.append(grouped)
+            cols = FEATURE_PASSES * P
+            for r in range(PACK):
+                quantise(
+                    grouped_tiles[r][:],
+                    codes[:, r * cols : (r + 1) * cols],
+                    scales[:, r * cols : (r + 1) * cols],
+                )
+            return codes, scales
+
+        z_codes, z_scales = quantise_row_tiles(z_raw, "z")
+        x_codes, x_scales = quantise_row_tiles(x_raw, "x")
+
+        raw_tiles = {}
+
+        def load_group(g):
+            first_node, count = groups[g]
+            rows = slice(first_node * P, (first_node + count) * P)
+            for name, matrix in (("v", V), ("w", W)):
+                raw = raw_pool.tile([P, GROUP_NODES * PROJECTED], BF16, name="raw_" + name, tag="raw_" + name)
+                nc.sync.dma_start(
+                    out=raw[:, : count * PROJECTED].rearrange("c (j k) -> c j k", j=count),
+                    in_=matrix[rows, :].rearrange("(j c) k -> c j k", c=P),
+                )
+                raw_tiles[(g, name)] = raw
+
+        for g in range(RAW_BUFS):
+            load_group(g)
+
+        th_cols = psum_words.tile([P, SAMPLE_TILES, P], BF16, name="th_cols", tag="bank")
+        for s in range(SAMPLE_TILES):
+            nc.tensor.transpose(th_cols[:, s, :], th_rows[:, s * P : (s + 1) * P], ident_bf16[:])
+        branch = consts.tile([P, SAMPLE_TILES, INNER_NODES, 2], F32, name="branch")
+        for side, sign in ((0, 0.5), (1, -0.5)):
+            nc.vector.tensor_scalar(
+                out=branch[:, :, :, side],
+                in0=th_cols[:, :, :INNER_NODES],
+                scalar1=sign,
+                scalar2=0.5,
+                op0=MULT,
+                op1=ADD,
+            )
+        prob = consts.tile([P, SAMPLE_TILES, NODES], F32, name="prob")
+        nc.vector.memset(prob[:, :, 0:1], 1.0)
+        first = 0
+        for depth in range(DEPTH):
+            width = 1 << depth
+            child = 2 * first + 1
+            nc.vector.tensor_tensor(
+                out=prob[:, :, child : child + 2 * width].rearrange("b s (i c) -> b s i c", c=2),
+                in0=branch[:, :, first : first + width, :],
+                in1=prob[:, :, first : first + width]
+                .unsqueeze(3)
+                .to_broadcast([P, SAMPLE_TILES, width, 2]),
+                op=MULT,
+            )
+            first = child
+
+        xq_codes = consts.tile([P, SAMPLES], U32, name="xq_codes", align_bytes=64)
+        xq_scales = consts.tile([P, SAMPLES], U8, name="xq_scales", align_bytes=64)
+        for s in range(SAMPLE_TILES):
+            xp = psum_products.tile([P, PACK, P], F32, name="xp", tag="wx")
+            for t in range(PACK):
+                for g in range(FEATURE_PASSES):
+                    z_cols = slice((t * FEATURE_PASSES + g) * P, (t * FEATURE_PASSES + g + 1) * P)
+                    x_cols = slice((s * FEATURE_PASSES + g) * P, (s * FEATURE_PASSES + g + 1) * P)
+                    nc.tensor.matmul_mx(
+                        out=xp[:, t, :],
+                        lhsT=z_codes[:, z_cols].bitcast(FP8X4),
+                        lhsT_scale=z_scales[:, z_cols],
+                        rhs=x_codes[:, x_cols].bitcast(FP8X4),
+                        rhs_scale=x_scales[:, x_cols],
+                        start=(g == 0),
+                        stop=(g == FEATURE_PASSES - 1),
+                    )
+            xp_grouped = first_stage.tile([P, P * PACK], BF16, name="xp_grouped", tag="xp_grouped", align_bytes=64)
+            nc.scalar.mul(
+                out=xp_grouped[:].rearrange("q (b t) -> q b t", t=PACK),
+                in_=xp[:].rearrange("q t b -> q b t"),
+                mul=1.0 / PROJECTED,
+            )
+            quantise(xp_grouped[:], xq_codes[:, s * P : (s + 1) * P], xq_scales[:, s * P : (s + 1) * P])
+
+        grouped_tiles = {}
+        code_tiles = {}
+        direct_products = {}
+        score = psum_score.tile([P, SAMPLES], F32, name="score")
+        sums = [
+            consts.tile([P, GROUP_NODES * CLASSES], F32, name="sum_%d" % s)
+            for s in range(DIRECT_TILES, SAMPLE_TILES)
+        ]
+
+        def transpose_group(g):
+            count = groups[g][1]
+            block_words = PROJECTED // 2
+            for name in ("v", "w"):
+                words = raw_tiles[(g, name)][:].bitcast(F32)
+                grouped = grouped_pool.tile([P, GROUP_NODES * PROJECTED], BF16, name="grouped_" + name, tag="grouped_" + name, align_bytes=64)
+                grouped_words = grouped[:].bitcast(F32)
+                for j in range(0, count, BANK_BLOCKS):
+                    blocks = min(BANK_BLOCKS, count - j)
+                    part = slice(j * block_words, (j + blocks) * block_words)
+                    transpose_blocks(words[:, part], blocks, grouped_words[:, part], nc.scalar.copy)
+                grouped_tiles[(g, name)] = grouped
+            if g + RAW_BUFS < len(groups):
+                load_group(g + RAW_BUFS)
+
+        def quantise_group(g):
+            count = groups[g][1]
+            for name in ("v", "w"):
+                codes = codes_pool.tile([P, GROUP_NODES * CLASSES], U32, name="codes_" + name, tag="codes_" + name, align_bytes=64)
+                scales = codes_pool.tile([P, GROUP_NODES * CLASSES], U8, name="scales_" + name, tag="scales_" + name, align_bytes=64)
+                quantise(
+                    grouped_tiles[(g, name)][:, : count * PROJECTED],
+                    codes[:, : count * CLASSES],
+                    scales[:, : count * CLASSES],
+                )
+                code_tiles[(g, name)] = (codes, scales)
+
+        def add_to_score(s, products, count, opens=False, closes=False):
+            for j in range(count):
+                nc.tensor.matmul(
+                    out=score[:, s * P : (s + 1) * P],
+                    lhsT=products[:, j * CLASSES : (j + 1) * CLASSES],
+                    rhs=ident_f32[:],
+                    is_transpose=True,
+                    start=(opens and j == 0),
+                    stop=(closes and j == count - 1),
+                )
+
+        def multiply_group(g):
+            first_node, count = groups[g]
+            cols = count * CLASSES
+            v_codes, v_scales = code_tiles[(g, "v")]
+            w_codes, w_scales = code_tiles[(g, "w")]
+            to_add = []
+            for s in range(SAMPLE_TILES):
+                samples = slice(s * P, (s + 1) * P)
+                vx = psum_products.tile([P, GROUP_NODES * CLASSES], F32, name="vx", tag="vx")
+                wx = psum_products.tile([P, GROUP_NODES * CLASSES], F32, name="wx", tag="wx")
+                for acc, codes, scales in ((vx, v_codes, v_scales), (wx, w_codes, w_scales)):
+                    nc.tensor.matmul_mx(
+                        out=acc[:, :cols],
+                        lhsT=xq_codes[:, samples].bitcast(FP8X4),
+                        lhsT_scale=xq_scales[:, samples],
+                        rhs=codes[:, :cols].bitcast(FP8X4),
+                        rhs_scale=scales[:, :cols],
+                        start=True,
+                        stop=True,
+                    )
+                tanh_vx = work.tile([P, GROUP_NODES * CLASSES], F32, name="tanh_vx", tag="tanh_vx")
+                nc.scalar.activation(out=tanh_vx[:, :cols], in_=vx[:, :cols], func=TANH)
+                if s < DIRECT_TILES:
+                    products = work.tile([P, GROUP_NODES * CLASSES], F32, name="direct", tag="direct")
+                    direct_products[(g, s)] = products
+                elif g == 0:
+                    products = sums[s - DIRECT_TILES]
+                else:
+                    products = work.tile([P, GROUP_NODES * CLASSES], F32, name="products", tag="products")
+                    to_add.append((s, products))
+                for j in range(count):
+                    node_cols = slice(j * CLASSES, (j + 1) * CLASSES)
+                    nc.vector.scalar_tensor_tensor(
+                        out=products[:, node_cols],
+                        in0=wx[:, node_cols],
+                        scalar=prob[:, s, first_node + j : first_node + j + 1],
+                        in1=tanh_vx[:, node_cols],
+                        op0=MULT,
+                        op1=MULT,
+                    )
+            for s, products in to_add:
+                total = sums[s - DIRECT_TILES]
+                nc.vector.tensor_tensor(out=total[:, :cols], in0=total[:, :cols], in1=products[:, :cols], op=ADD)
+
+        def add_direct_products(g):
+            for s in range(DIRECT_TILES):
+                add_to_score(s, direct_products[(g, s)], groups[g][1], opens=(g == 0 and s == 0))
+
+        transpose_group(0)
+        transpose_group(1)
+        quantise_group(0)
+        for g in range(len(groups)):
+            if g + 1 < len(groups):
+                quantise_group(g + 1)
+            multiply_group(g)
+            if g + 2 < len(groups):
+                transpose_group(g + 2)
+            add_direct_products(g)
+        for s in range(DIRECT_TILES, SAMPLE_TILES):
+            add_to_score(s, sums[s - DIRECT_TILES], GROUP_NODES, closes=(s == SAMPLE_TILES - 1))
+
+        result = consts.tile([P, SAMPLES], F32, name="result")
+        nc.scalar.copy(out=result[:], in_=score[:])
+        nc.sync.dma_start(out=out, in_=result[:])

@@ -26,7 +26,7 @@ FEATURE_PASSES = FEATURES // K_PASS
 GROUP_NODES = 4
 BANK_BLOCKS = 2
 
-DIRECT_TILES = 2
+DIRECT_TILES = 4
 RAW_BUFS = 6
 
 FLOPS = 2 * PROJECTED * SAMPLES * FEATURES + 2 * 2 * NODES * CLASSES * SAMPLES * PROJECTED
@@ -290,7 +290,13 @@ def tile_bonsailayer_pa_kernel(tc, X, Z, W, V, th, out):
 
         def add_direct_products(g):
             for s in range(DIRECT_TILES):
-                add_to_score(s, direct_products[(g, s)], groups[g][1], opens=(g == 0 and s == 0))
+                add_to_score(
+                    s,
+                    direct_products[(g, s)],
+                    groups[g][1],
+                    opens=(g == 0 and s == 0),
+                    closes=(DIRECT_TILES == SAMPLE_TILES and g == len(groups) - 1 and s == SAMPLE_TILES - 1),
+                )
 
         transpose_group(0)
         transpose_group(1)

@@ -26,7 +26,9 @@ FEATURE_PASSES = FEATURES // K_PASS
 GROUP_NODES = 4
 BANK_BLOCKS = 2
 
-DIRECT_TILES = 4
+STEP_TILES = 2
+STEPS = SAMPLE_TILES // STEP_TILES
+MATRICES = ("v", "w")
 RAW_BUFS = 6
 
 FLOPS = 2 * PROJECTED * SAMPLES * FEATURES + 2 * 2 * NODES * CLASSES * SAMPLES * PROJECTED
@@ -129,19 +131,19 @@ def tile_bonsailayer_pa_kernel(tc, X, Z, W, V, th, out):
 
         raw_tiles = {}
 
-        def load_group(g):
+        def load_matrix(g, name):
             first_node, count = groups[g]
-            rows = slice(first_node * P, (first_node + count) * P)
-            for name, matrix in (("v", V), ("w", W)):
-                raw = raw_pool.tile([P, GROUP_NODES * PROJECTED], BF16, name="raw_" + name, tag="raw_" + name)
-                nc.sync.dma_start(
-                    out=raw[:, : count * PROJECTED].rearrange("c (j k) -> c j k", j=count),
-                    in_=matrix[rows, :].rearrange("(j c) k -> c j k", c=P),
-                )
-                raw_tiles[(g, name)] = raw
+            matrix = V if name == "v" else W
+            raw = raw_pool.tile([P, GROUP_NODES * PROJECTED], BF16, name="raw_" + name, tag="raw_" + name)
+            nc.sync.dma_start(
+                out=raw[:, : count * PROJECTED].rearrange("c (j k) -> c j k", j=count),
+                in_=matrix[first_node * P : (first_node + count) * P, :].rearrange("(j c) k -> c j k", c=P),
+            )
+            raw_tiles[(g, name)] = raw
 
         for g in range(RAW_BUFS):
-            load_group(g)
+            for name in MATRICES:
+                load_matrix(g, name)
 
         th_cols = psum_words.tile([P, SAMPLE_TILES, P], BF16, name="th_cols", tag="bank")
         for s in range(SAMPLE_TILES):
@@ -199,39 +201,33 @@ def tile_bonsailayer_pa_kernel(tc, X, Z, W, V, th, out):
 
         grouped_tiles = {}
         code_tiles = {}
-        direct_products = {}
         score = psum_score.tile([P, SAMPLES], F32, name="score")
-        sums = [
-            consts.tile([P, GROUP_NODES * CLASSES], F32, name="sum_%d" % s)
-            for s in range(DIRECT_TILES, SAMPLE_TILES)
-        ]
+        sums = [consts.tile([P, GROUP_NODES * CLASSES], F32, name="sum_%d" % h) for h in range(STEPS)]
 
-        def transpose_group(g):
+        def transpose_matrix(g, name):
             count = groups[g][1]
             block_words = PROJECTED // 2
-            for name in ("v", "w"):
-                words = raw_tiles[(g, name)][:].bitcast(F32)
-                grouped = grouped_pool.tile([P, GROUP_NODES * PROJECTED], BF16, name="grouped_" + name, tag="grouped_" + name, align_bytes=64)
-                grouped_words = grouped[:].bitcast(F32)
-                for j in range(0, count, BANK_BLOCKS):
-                    blocks = min(BANK_BLOCKS, count - j)
-                    part = slice(j * block_words, (j + blocks) * block_words)
-                    transpose_blocks(words[:, part], blocks, grouped_words[:, part], nc.scalar.copy)
-                grouped_tiles[(g, name)] = grouped
+            words = raw_tiles[(g, name)][:].bitcast(F32)
+            grouped = grouped_pool.tile([P, GROUP_NODES * PROJECTED], BF16, name="grouped_" + name, tag="grouped_" + name, align_bytes=64)
+            grouped_words = grouped[:].bitcast(F32)
+            for j in range(0, count, BANK_BLOCKS):
+                blocks = min(BANK_BLOCKS, count - j)
+                part = slice(j * block_words, (j + blocks) * block_words)
+                transpose_blocks(words[:, part], blocks, grouped_words[:, part], nc.scalar.copy)
+            grouped_tiles[(g, name)] = grouped
             if g + RAW_BUFS < len(groups):
-                load_group(g + RAW_BUFS)
+                load_matrix(g + RAW_BUFS, name)
 
-        def quantise_group(g):
+        def quantise_matrix(g, name):
             count = groups[g][1]
-            for name in ("v", "w"):
-                codes = codes_pool.tile([P, GROUP_NODES * CLASSES], U32, name="codes_" + name, tag="codes_" + name, align_bytes=64)
-                scales = codes_pool.tile([P, GROUP_NODES * CLASSES], U8, name="scales_" + name, tag="scales_" + name, align_bytes=64)
-                quantise(
-                    grouped_tiles[(g, name)][:, : count * PROJECTED],
-                    codes[:, : count * CLASSES],
-                    scales[:, : count * CLASSES],
-                )
-                code_tiles[(g, name)] = (codes, scales)
+            codes = codes_pool.tile([P, GROUP_NODES * CLASSES], U32, name="codes_" + name, tag="codes_" + name, align_bytes=64)
+            scales = codes_pool.tile([P, GROUP_NODES * CLASSES], U8, name="scales_" + name, tag="scales_" + name, align_bytes=64)
+            quantise(
+                grouped_tiles[(g, name)][:, : count * PROJECTED],
+                codes[:, : count * CLASSES],
+                scales[:, : count * CLASSES],
+            )
+            code_tiles[(g, name)] = (codes, scales)
 
         def add_to_score(s, products, count, opens=False, closes=False):
             for j in range(count):
@@ -244,72 +240,74 @@ def tile_bonsailayer_pa_kernel(tc, X, Z, W, V, th, out):
                     stop=(closes and j == count - 1),
                 )
 
-        def multiply_group(g):
+        def multiply_step(g, h):
             first_node, count = groups[g]
             cols = count * CLASSES
-            v_codes, v_scales = code_tiles[(g, "v")]
-            w_codes, w_scales = code_tiles[(g, "w")]
-            to_add = []
-            for s in range(SAMPLE_TILES):
-                samples = slice(s * P, (s + 1) * P)
-                vx = psum_products.tile([P, GROUP_NODES * CLASSES], F32, name="vx", tag="vx")
-                wx = psum_products.tile([P, GROUP_NODES * CLASSES], F32, name="wx", tag="wx")
-                for acc, codes, scales in ((vx, v_codes, v_scales), (wx, w_codes, w_scales)):
+            tiles = range(h * STEP_TILES, (h + 1) * STEP_TILES)
+            accs = {}
+            for name in MATRICES:
+                codes, scales = code_tiles[(g, name)]
+                for s in tiles:
+                    acc = psum_products.tile([P, GROUP_NODES * CLASSES], F32, name=name + "x", tag=name + "x")
                     nc.tensor.matmul_mx(
                         out=acc[:, :cols],
-                        lhsT=xq_codes[:, samples].bitcast(FP8X4),
-                        lhsT_scale=xq_scales[:, samples],
+                        lhsT=xq_codes[:, s * P : (s + 1) * P].bitcast(FP8X4),
+                        lhsT_scale=xq_scales[:, s * P : (s + 1) * P],
                         rhs=codes[:, :cols].bitcast(FP8X4),
                         rhs_scale=scales[:, :cols],
                         start=True,
                         stop=True,
                     )
+                    accs[(name, s)] = acc
+            step_products = []
+            for s in tiles:
                 tanh_vx = work.tile([P, GROUP_NODES * CLASSES], F32, name="tanh_vx", tag="tanh_vx")
-                nc.scalar.activation(out=tanh_vx[:, :cols], in_=vx[:, :cols], func=TANH)
-                if s < DIRECT_TILES:
-                    products = work.tile([P, GROUP_NODES * CLASSES], F32, name="direct", tag="direct")
-                    direct_products[(g, s)] = products
-                elif g == 0:
-                    products = sums[s - DIRECT_TILES]
+                nc.scalar.activation(out=tanh_vx[:, :cols], in_=accs[("v", s)][:, :cols], func=TANH)
+                if g == 0 and s % 2 == 1:
+                    products = sums[h]
                 else:
-                    products = work.tile([P, GROUP_NODES * CLASSES], F32, name="products", tag="products")
-                    to_add.append((s, products))
+                    products = work.tile([P, GROUP_NODES * CLASSES], F32, name="products", tag="products", bufs=6)
                 for j in range(count):
                     node_cols = slice(j * CLASSES, (j + 1) * CLASSES)
                     nc.vector.scalar_tensor_tensor(
                         out=products[:, node_cols],
-                        in0=wx[:, node_cols],
+                        in0=accs[("w", s)][:, node_cols],
                         scalar=prob[:, s, first_node + j : first_node + j + 1],
                         in1=tanh_vx[:, node_cols],
                         op0=MULT,
                         op1=MULT,
                     )
-            for s, products in to_add:
-                total = sums[s - DIRECT_TILES]
-                nc.vector.tensor_tensor(out=total[:, :cols], in0=total[:, :cols], in1=products[:, :cols], op=ADD)
+                step_products.append(products)
+            return step_products
 
-        def add_direct_products(g):
-            for s in range(DIRECT_TILES):
-                add_to_score(
-                    s,
-                    direct_products[(g, s)],
-                    groups[g][1],
-                    opens=(g == 0 and s == 0),
-                    closes=(DIRECT_TILES == SAMPLE_TILES and g == len(groups) - 1 and s == SAMPLE_TILES - 1),
+        def add_step(g, h, step_products):
+            count = groups[g][1]
+            cols = count * CLASSES
+            add_to_score(h * STEP_TILES, step_products[0], count, opens=(g == 0 and h == 0))
+            if g > 0:
+                nc.vector.tensor_tensor(
+                    out=sums[h][:, :cols], in0=sums[h][:, :cols], in1=step_products[1][:, :cols], op=ADD
                 )
 
-        transpose_group(0)
-        transpose_group(1)
-        quantise_group(0)
+        for g in range(2):
+            for name in MATRICES:
+                transpose_matrix(g, name)
+        for name in MATRICES:
+            quantise_matrix(0, name)
+        earlier = None
         for g in range(len(groups)):
-            if g + 1 < len(groups):
-                quantise_group(g + 1)
-            multiply_group(g)
-            if g + 2 < len(groups):
-                transpose_group(g + 2)
-            add_direct_products(g)
-        for s in range(DIRECT_TILES, SAMPLE_TILES):
-            add_to_score(s, sums[s - DIRECT_TILES], GROUP_NODES, closes=(s == SAMPLE_TILES - 1))
+            for h in range(STEPS):
+                if g + 1 < len(groups):
+                    quantise_matrix(g + 1, MATRICES[h])
+                step_products = multiply_step(g, h)
+                if g + 2 < len(groups):
+                    transpose_matrix(g + 2, MATRICES[h])
+                if earlier is not None:
+                    add_step(*earlier)
+                earlier = (g, h, step_products)
+        add_step(*earlier)
+        for h in range(STEPS):
+            add_to_score(h * STEP_TILES + 1, sums[h], GROUP_NODES, closes=(h == STEPS - 1))
 
         result = consts.tile([P, SAMPLES], F32, name="result")
         nc.scalar.copy(out=result[:], in_=score[:])

@@ -285,7 +285,7 @@ def tile_bonsailayer_pa_kernel(tc, X, Z, W, V, th, out):
             cols = count * CLASSES
             add_to_score(h * STEP_TILES, step_products[0], count, opens=(g == 0 and h == 0))
             if g > 0:
-                nc.vector.tensor_tensor(
+                nc.gpsimd.tensor_tensor(
                     out=sums[h][:, :cols], in0=sums[h][:, :cols], in1=step_products[1][:, :cols], op=ADD
                 )
 

@@ -202,7 +202,7 @@ def tile_bonsailayer_pa_kernel(tc, X, Z, W, V, th, out):
         grouped_tiles = {}
         code_tiles = {}
         score = psum_score.tile([P, SAMPLES], F32, name="score")
-        sums = [consts.tile([P, GROUP_NODES * CLASSES], F32, name="sum_%d" % h) for h in range(STEPS)]
+        sums = [consts.tile([P, GROUP_NODES * CLASSES], F32, name="sum_%d" % s) for s in range(SAMPLE_TILES)]
 
         def transpose_matrix(g, name):
             count = groups[g][1]
@@ -263,8 +263,8 @@ def tile_bonsailayer_pa_kernel(tc, X, Z, W, V, th, out):
             for s in tiles:
                 tanh_vx = work.tile([P, GROUP_NODES * CLASSES], F32, name="tanh_vx", tag="tanh_vx")
                 nc.scalar.activation(out=tanh_vx[:, :cols], in_=accs[("v", s)][:, :cols], func=TANH)
-                if g == 0 and s % 2 == 1:
-                    products = sums[h]
+                if g == 0:
+                    products = sums[s]
                 else:
                     products = work.tile([P, GROUP_NODES * CLASSES], F32, name="products", tag="products", bufs=6)
                 for j in range(count):
@@ -281,13 +281,9 @@ def tile_bonsailayer_pa_kernel(tc, X, Z, W, V, th, out):
             return step_products
 
         def add_step(g, h, step_products):
-            count = groups[g][1]
-            cols = count * CLASSES
-            add_to_score(h * STEP_TILES, step_products[0], count, opens=(g == 0 and h == 0))
-            if g > 0:
-                nc.gpsimd.tensor_tensor(
-                    out=sums[h][:, :cols], in0=sums[h][:, :cols], in1=step_products[1][:, :cols], op=ADD
-                )
+            cols = groups[g][1] * CLASSES
+            for engine, s, products in zip((nc.vector, nc.gpsimd), range(h * STEP_TILES, (h + 1) * STEP_TILES), step_products):
+                engine.tensor_tensor(out=sums[s][:, :cols], in0=sums[s][:, :cols], in1=products[:, :cols], op=ADD)
 
         for g in range(2):
             for name in MATRICES:
@@ -304,10 +300,10 @@ def tile_bonsailayer_pa_kernel(tc, X, Z, W, V, th, out):
                     transpose_matrix(g + 2, MATRICES[h])
                 if earlier is not None:
                     add_step(*earlier)
-                earlier = (g, h, step_products)
+                earlier = (g, h, step_products) if g > 0 else None
         add_step(*earlier)
-        for h in range(STEPS):
-            add_to_score(h * STEP_TILES + 1, sums[h], GROUP_NODES, closes=(h == STEPS - 1))
+        for s in range(SAMPLE_TILES):
+            add_to_score(s, sums[s], GROUP_NODES, opens=(s == 0), closes=(s == SAMPLE_TILES - 1))
 
         result = consts.tile([P, SAMPLES], F32, name="result")
         nc.scalar.copy(out=result[:], in_=score[:])

@@ -202,7 +202,7 @@ def tile_bonsailayer_pa_kernel(tc, X, Z, W, V, th, out):
         grouped_tiles = {}
         code_tiles = {}
         score = psum_score.tile([P, SAMPLES], F32, name="score")
-        sums = [consts.tile([P, GROUP_NODES * CLASSES], F32, name="sum_%d" % s) for s in range(SAMPLE_TILES)]
+        sums = [consts.tile([P, GROUP_NODES * CLASSES], F32, name="sum_%d" % h) for h in range(STEPS)]
 
         def transpose_matrix(g, name):
             count = groups[g][1]
@@ -210,10 +210,14 @@ def tile_bonsailayer_pa_kernel(tc, X, Z, W, V, th, out):
             words = raw_tiles[(g, name)][:].bitcast(F32)
             grouped = grouped_pool.tile([P, GROUP_NODES * PROJECTED], BF16, name="grouped_" + name, tag="grouped_" + name, align_bytes=64)
             grouped_words = grouped[:].bitcast(F32)
-            for j in range(0, count, BANK_BLOCKS):
-                blocks = min(BANK_BLOCKS, count - j)
+            scalar_blocks = count - 1 if count == GROUP_NODES else count
+            for j in range(0, scalar_blocks, BANK_BLOCKS):
+                blocks = min(BANK_BLOCKS, scalar_blocks - j)
                 part = slice(j * block_words, (j + blocks) * block_words)
                 transpose_blocks(words[:, part], blocks, grouped_words[:, part], nc.scalar.copy)
+            for j in range(scalar_blocks, count):
+                part = slice(j * block_words, (j + 1) * block_words)
+                transpose_blocks(words[:, part], 1, grouped_words[:, part], nc.vector.tensor_copy)
             grouped_tiles[(g, name)] = grouped
             if g + RAW_BUFS < len(groups):
                 load_matrix(g + RAW_BUFS, name)
@@ -263,8 +267,8 @@ def tile_bonsailayer_pa_kernel(tc, X, Z, W, V, th, out):
             for s in tiles:
                 tanh_vx = work.tile([P, GROUP_NODES * CLASSES], F32, name="tanh_vx", tag="tanh_vx")
                 nc.scalar.activation(out=tanh_vx[:, :cols], in_=accs[("v", s)][:, :cols], func=TANH)
-                if g == 0:
-                    products = sums[s]
+                if g == 0 and s % 2 == 1:
+                    products = sums[h]
                 else:
                     products = work.tile([P, GROUP_NODES * CLASSES], F32, name="products", tag="products", bufs=6)
                 for j in range(count):
@@ -281,9 +285,13 @@ def tile_bonsailayer_pa_kernel(tc, X, Z, W, V, th, out):
             return step_products
 
         def add_step(g, h, step_products):
-            cols = groups[g][1] * CLASSES
-            for engine, s, products in zip((nc.vector, nc.gpsimd), range(h * STEP_TILES, (h + 1) * STEP_TILES), step_products):
-                engine.tensor_tensor(out=sums[s][:, :cols], in0=sums[s][:, :cols], in1=products[:, :cols], op=ADD)
+            count = groups[g][1]
+            cols = count * CLASSES
+            add_to_score(h * STEP_TILES, step_products[0], count, opens=(g == 0 and h == 0))
+            if g > 0:
+                nc.gpsimd.tensor_tensor(
+                    out=sums[h][:, :cols], in0=sums[h][:, :cols], in1=step_products[1][:, :cols], op=ADD
+                )
 
         for g in range(2):
             for name in MATRICES:
@@ -300,10 +308,10 @@ def tile_bonsailayer_pa_kernel(tc, X, Z, W, V, th, out):
                     transpose_matrix(g + 2, MATRICES[h])
                 if earlier is not None:
                     add_step(*earlier)
-                earlier = (g, h, step_products) if g > 0 else None
+                earlier = (g, h, step_products)
         add_step(*earlier)
-        for s in range(SAMPLE_TILES):
-            add_to_score(s, sums[s], GROUP_NODES, opens=(s == 0), closes=(s == SAMPLE_TILES - 1))
+        for h in range(STEPS):
+            add_to_score(h * STEP_TILES + 1, sums[h], GROUP_NODES, closes=(h == STEPS - 1))
 
         result = consts.tile([P, SAMPLES], F32, name="result")
         nc.scalar.copy(out=result[:], in_=score[:])

from contextlib import ExitStack

import concourse.mybir as mybir
from concourse.masks import make_identity

F32 = mybir.dt.float32
BF16 = mybir.dt.bfloat16
U32 = mybir.dt.uint32
U8 = mybir.dt.uint8
FP8X4 = mybir.dt.float8_e4m3fn_x4
ADD = mybir.AluOpType.add
MULT = mybir.AluOpType.mult
TANH = mybir.ActivationFunctionType.Tanh

P = 128
PACK = 4
K_PASS = P * PACK
HALVES = 2

SAMPLES, FEATURES, PROJECTED, CLASSES = 512, 1024, 512, 128
DEPTH = 5
INNER_NODES = (1 << DEPTH) - 1
NODES = 2 * INNER_NODES + 1
SAMPLE_TILES = SAMPLES // P
FEATURE_PASSES = FEATURES // K_PASS
GROUP_NODES = 4
BANK_BLOCKS = 2

STEP_TILES = 2
STEPS = SAMPLE_TILES // STEP_TILES
MATRICES = ("v", "w")
RAW_BUFS = 6

FLOPS = 2 * PROJECTED * SAMPLES * FEATURES + 2 * 2 * NODES * CLASSES * SAMPLES * PROJECTED


def node_groups():
    groups = []
    first = 0
    for size in (GROUP_NODES, 2, 1):
        for repeat in range((NODES - first) // size):
            groups.append((first, size))
            first += size
    return groups


def tile_bonsailayer_pa_kernel(tc, X, Z, W, V, th, out):
    nc = tc.nc
    groups = node_groups()

    with ExitStack() as ctx:
        consts = ctx.enter_context(tc.tile_pool(name="consts", bufs=1))
        first_stage = ctx.enter_context(tc.tile_pool(name="first_stage", bufs=4))
        raw_pool = ctx.enter_context(tc.tile_pool(name="raw", bufs=RAW_BUFS))
        grouped_pool = ctx.enter_context(tc.tile_pool(name="grouped", bufs=3))
        codes_pool = ctx.enter_context(tc.tile_pool(name="codes", bufs=3))
        work = ctx.enter_context(tc.tile_pool(name="work", bufs=4))
        psum_words = ctx.enter_context(tc.psum_pool(name="psum_words", bufs=3))
        psum_products = ctx.enter_context(tc.psum_pool(name="psum_products", bufs=2))
        psum_score = ctx.enter_context(tc.psum_pool(name="psum_score", bufs=1))
        ctx.enter_context(tc.manual_schedule())

        ident_f32 = consts.tile([P, P], F32, name="ident_f32")
        make_identity(nc, ident_f32[:])
        ident_bf16 = consts.tile([P, P], BF16, name="ident_bf16")
        make_identity(nc, ident_bf16[:])

        th_rows = consts.tile([P, SAMPLES], BF16, name="th_rows")
        nc.vector.memset(th_rows[:], 0.0)
        nc.scalar.dma_start(out=th_rows[:INNER_NODES, :], in_=th)

        warm = consts.tile([P, 1], F32, name="warm")
        nc.vector.memset(warm[:], 0.0)
        nc.scalar.activation(out=warm[:], in_=warm[:], func=TANH)

        z_raw = consts.tile([P, PACK * FEATURES], BF16, name="z_raw")
        for u in range(HALVES):
            nc.sync.dma_start(
                out=z_raw[:, u * 2 * FEATURES : (u + 1) * 2 * FEATURES],
                in_=Z[u * 2 * P : (u + 1) * 2 * P, :].rearrange("(q e) d -> q (e d)", e=2),
            )
        x_raw = consts.tile([P, SAMPLE_TILES * FEATURES], BF16, name="x_raw")
        for s in range(SAMPLE_TILES):
            nc.sync.dma_start(
                out=x_raw[:, s * FEATURES : (s + 1) * FEATURES], in_=X[s * P : (s + 1) * P, :]
            )

        def transpose_blocks(words, blocks, grouped_words, copy):
            bank = psum_words.tile([P, BANK_BLOCKS, HALVES, P], F32, name="bank", tag="bank")
            for a in range(blocks):
                for u in range(HALVES):
                    first_word = (a * HALVES + u) * P
                    nc.tensor.transpose(
                        bank[:, a, u, :], words[:, first_word : first_word + P], ident_f32[:]
                    )
            copy(
                out=grouped_words.rearrange("q (a r u) -> q a r u", a=blocks, u=HALVES),
                in_=bank[:, :blocks].rearrange("q a u r -> q a r u"),
            )

        def quantise(grouped, codes, scales):
            nc.vector.quantize_mx(out=codes.bitcast(FP8X4), scales=scales, in_=grouped)

        def quantise_row_tiles(raw, name):
            codes = consts.tile([P, PACK * FEATURE_PASSES * P], U32, name=name + "_codes", align_bytes=64)
            scales = consts.tile([P, PACK * FEATURE_PASSES * P], U8, name=name + "_scales", align_bytes=64)
            words = raw[:].bitcast(F32)
            row_words = FEATURES // 2
            grouped_tiles = []
            for r in range(PACK):
                grouped = first_stage.tile([P, FEATURES], BF16, name=name + "_grouped", tag="grouped", align_bytes=64)
                copy = nc.scalar.copy if r % 2 == 0 else nc.vector.tensor_copy
                transpose_blocks(
                    words[:, r * row_words : (r + 1) * row_words],
                    FEATURE_PASSES,
                    grouped[:].bitcast(F32),
                    copy,
                )
                grouped_tiles.append(grouped)
            cols = FEATURE_PASSES * P
            for r in range(PACK):
                quantise(
                    grouped_tiles[r][:],
                    codes[:, r * cols : (r + 1) * cols],
                    scales[:, r * cols : (r + 1) * cols],
                )
            return codes, scales

        z_codes, z_scales = quantise_row_tiles(z_raw, "z")
        x_codes, x_scales = quantise_row_tiles(x_raw, "x")

        raw_tiles = {}

        def load_matrix(g, name):
            first_node, count = groups[g]
            matrix = V if name == "v" else W
            raw = raw_pool.tile([P, GROUP_NODES * PROJECTED], BF16, name="raw_" + name, tag="raw_" + name)
            nc.sync.dma_start(
                out=raw[:, : count * PROJECTED].rearrange("c (j k) -> c j k", j=count),
                in_=matrix[first_node * P : (first_node + count) * P, :].rearrange("(j c) k -> c j k", c=P),
            )
            raw_tiles[(g, name)] = raw

        for g in range(RAW_BUFS):
            for name in MATRICES:
                load_matrix(g, name)

        th_cols = psum_words.tile([P, SAMPLE_TILES, P], BF16, name="th_cols", tag="bank")
        for s in range(SAMPLE_TILES):
            nc.tensor.transpose(th_cols[:, s, :], th_rows[:, s * P : (s + 1) * P], ident_bf16[:])
        branch = consts.tile([P, SAMPLE_TILES, INNER_NODES, 2], F32, name="branch")
        for side, sign in ((0, 0.5), (1, -0.5)):
            nc.vector.tensor_scalar(
                out=branch[:, :, :, side],
                in0=th_cols[:, :, :INNER_NODES],
                scalar1=sign,
                scalar2=0.5,
                op0=MULT,
                op1=ADD,
            )
        prob = consts.tile([P, SAMPLE_TILES, NODES], F32, name="prob")
        nc.vector.memset(prob[:, :, 0:1], 1.0)
        first = 0
        for depth in range(DEPTH):
            width = 1 << depth
            child = 2 * first + 1
            nc.vector.tensor_tensor(
                out=prob[:, :, child : child + 2 * width].rearrange("b s (i c) -> b s i c", c=2),
                in0=branch[:, :, first : first + width, :],
                in1=prob[:, :, first : first + width]
                .unsqueeze(3)
                .to_broadcast([P, SAMPLE_TILES, width, 2]),
                op=MULT,
            )
            first = child

        xq_codes = consts.tile([P, SAMPLES], U32, name="xq_codes", align_bytes=64)
        xq_scales = consts.tile([P, SAMPLES], U8, name="xq_scales", align_bytes=64)
        for s in range(SAMPLE_TILES):
            xp = psum_products.tile([P, PACK, P], F32, name="xp", tag="wx")
            for t in range(PACK):
                for g in range(FEATURE_PASSES):
                    z_cols = slice((t * FEATURE_PASSES + g) * P, (t * FEATURE_PASSES + g + 1) * P)
                    x_cols = slice((s * FEATURE_PASSES + g) * P, (s * FEATURE_PASSES + g + 1) * P)
                    nc.tensor.matmul_mx(
                        out=xp[:, t, :],
                        lhsT=z_codes[:, z_cols].bitcast(FP8X4),
                        lhsT_scale=z_scales[:, z_cols],
                        rhs=x_codes[:, x_cols].bitcast(FP8X4),
                        rhs_scale=x_scales[:, x_cols],
                        start=(g == 0),
                        stop=(g == FEATURE_PASSES - 1),
                    )
            xp_grouped = first_stage.tile([P, P * PACK], BF16, name="xp_grouped", tag="xp_grouped", align_bytes=64)
            nc.scalar.mul(
                out=xp_grouped[:].rearrange("q (b t) -> q b t", t=PACK),
                in_=xp[:].rearrange("q t b -> q b t"),
                mul=1.0 / PROJECTED,
            )
            quantise(xp_grouped[:], xq_codes[:, s * P : (s + 1) * P], xq_scales[:, s * P : (s + 1) * P])

        grouped_tiles = {}
        code_tiles = {}
        score = psum_score.tile([P, SAMPLES], F32, name="score")
        sums = [consts.tile([P, GROUP_NODES * CLASSES], F32, name="sum_%d" % h) for h in range(STEPS)]

        def transpose_matrix(g, name):
            count = groups[g][1]
            block_words = PROJECTED // 2
            words = raw_tiles[(g, name)][:].bitcast(F32)
            grouped = grouped_pool.tile([P, GROUP_NODES * PROJECTED], BF16, name="grouped_" + name, tag="grouped_" + name, align_bytes=64)
            grouped_words = grouped[:].bitcast(F32)
            scalar_blocks = count - 1 if count == GROUP_NODES else count
            for j in range(0, scalar_blocks, BANK_BLOCKS):
                blocks = min(BANK_BLOCKS, scalar_blocks - j)
                part = slice(j * block_words, (j + blocks) * block_words)
                transpose_blocks(words[:, part], blocks, grouped_words[:, part], nc.scalar.copy)
            for j in range(scalar_blocks, count):
                part = slice(j * block_words, (j + 1) * block_words)
                transpose_blocks(words[:, part], 1, grouped_words[:, part], nc.vector.tensor_copy)
            grouped_tiles[(g, name)] = grouped
            if g + RAW_BUFS < len(groups):
                load_matrix(g + RAW_BUFS, name)

        def quantise_matrix(g, name):
            count = groups[g][1]
            codes = codes_pool.tile([P, GROUP_NODES * CLASSES], U32, name="codes_" + name, tag="codes_" + name, align_bytes=64)
            scales = codes_pool.tile([P, GROUP_NODES * CLASSES], U8, name="scales_" + name, tag="scales_" + name, align_bytes=64)
            quantise(
                grouped_tiles[(g, name)][:, : count * PROJECTED],
                codes[:, : count * CLASSES],
                scales[:, : count * CLASSES],
            )
            code_tiles[(g, name)] = (codes, scales)

        def add_to_score(s, products, count, opens=False, closes=False):
            for j in range(count):
                nc.tensor.matmul(
                    out=score[:, s * P : (s + 1) * P],
                    lhsT=products[:, j * CLASSES : (j + 1) * CLASSES],
                    rhs=ident_f32[:],
                    is_transpose=True,
                    start=(opens and j == 0),
                    stop=(closes and j == count - 1),
                )

        def multiply_step(g, h):
            first_node, count = groups[g]
            cols = count * CLASSES
            tiles = range(h * STEP_TILES, (h + 1) * STEP_TILES)
            accs = {}
            for name in MATRICES:
                codes, scales = code_tiles[(g, name)]
                for s in tiles:
                    acc = psum_products.tile([P, GROUP_NODES * CLASSES], F32, name=name + "x", tag=name + "x")
                    nc.tensor.matmul_mx(
                        out=acc[:, :cols],
                        lhsT=xq_codes[:, s * P : (s + 1) * P].bitcast(FP8X4),
                        lhsT_scale=xq_scales[:, s * P : (s + 1) * P],
                        rhs=codes[:, :cols].bitcast(FP8X4),
                        rhs_scale=scales[:, :cols],
                        start=True,
                        stop=True,
                    )
                    accs[(name, s)] = acc
            step_products = []
            for s in tiles:
                tanh_vx = work.tile([P, GROUP_NODES * CLASSES], F32, name="tanh_vx", tag="tanh_vx")
                nc.scalar.activation(out=tanh_vx[:, :cols], in_=accs[("v", s)][:, :cols], func=TANH)
                if g == 0 and s % 2 == 1:
                    products = sums[h]
                else:
                    products = work.tile([P, GROUP_NODES * CLASSES], F32, name="products", tag="products", bufs=6)
                for j in range(count):
                    node_cols = slice(j * CLASSES, (j + 1) * CLASSES)
                    nc.vector.scalar_tensor_tensor(
                        out=products[:, node_cols],
                        in0=accs[("w", s)][:, node_cols],
                        scalar=prob[:, s, first_node + j : first_node + j + 1],
                        in1=tanh_vx[:, node_cols],
                        op0=MULT,
                        op1=MULT,
                    )
                step_products.append(products)
            return step_products

        def add_step(g, h, step_products):
            count = groups[g][1]
            cols = count * CLASSES
            add_to_score(h * STEP_TILES, step_products[0], count, opens=(g == 0 and h == 0))
            if g > 0:
                nc.gpsimd.tensor_tensor(
                    out=sums[h][:, :cols], in0=sums[h][:, :cols], in1=step_products[1][:, :cols], op=ADD
                )

        for g in range(2):
            for name in MATRICES:
                transpose_matrix(g, name)
        for name in MATRICES:
            quantise_matrix(0, name)
        earlier = None
        for g in range(len(groups)):
            for h in range(STEPS):
                if g + 1 < len(groups):
                    quantise_matrix(g + 1, MATRICES[h])
                step_products = multiply_step(g, h)
                if g + 2 < len(groups):
                    transpose_matrix(g + 2, MATRICES[h])
                if earlier is not None:
                    add_step(*earlier)
                earlier = (g, h, step_products)
        add_step(*earlier)
        for h in range(STEPS):
            add_to_score(h * STEP_TILES + 1, sums[h], GROUP_NODES, closes=(h == STEPS - 1))

        result = consts.tile([P, SAMPLES], F32, name="result")
        nc.scalar.copy(out=result[:], in_=score[:])
        nc.sync.dma_start(out=out, in_=result[:])
